import numpy as np
import ml_dtypes

BF16 = ml_dtypes.bfloat16


def bf(x):
    return np.asarray(x, np.float32).astype(BF16)


def f32(x):
    return np.asarray(x, np.float32)


def f64(x):
    return np.asarray(x).astype(np.float64)


def striped(idx):
    return np.tile(idx.reshape(-1, 16).T, (8, 1))


E, V, B, T, H, D, N, RUN, K = 512, 512, 4, 512, 4, 128, 2048, 256, 8


def positional():
    position = np.arange(T, dtype=np.float32)[:, None]
    rate = np.exp(f64(np.arange(0, E, 2, dtype=np.float32) * np.float32(-np.log(10000.0) / E))).astype(np.float32)
    angle = f64(position * rate[None, :])
    pe = np.zeros((T, E))
    pe[:, 0::2] = np.sin(angle)
    pe[:, 1::2] = np.cos(angle)
    return pe


def setup_inputs():
    s = 1.0 / np.sqrt(E)
    return {
        "table": f32(np.random.standard_normal((E, V))),
        "pos": f32(np.tile(positional().T, (1, B))),
        "wq": bf(np.random.standard_normal((E, E)) * s),
        "bq": f32(0.3 * np.random.standard_normal((E, 1))),
        "wk": bf(np.random.standard_normal((E, E)) * s),
        "wv": bf(np.random.standard_normal((E, E)) * s),
        "bv": f32(0.3 * np.random.standard_normal((E, 1))),
        "wo": bf(np.random.standard_normal((E, E)) * s),
        "bo": f32(0.3 * np.random.standard_normal((E, 1))),
        "offs": striped(np.concatenate([np.random.permutation(V)[:RUN] for _ in range(K)])),
    }


def reference(table, pos, wq, bq, wk, wv, bv, wo, bo, offs):
    idx = offs[:16].T.reshape(-1)
    x = f64(table)[:, idx] + f64(pos)
    qry = f64(wq).T @ x + f64(bq)
    key = f64(wk).T @ x
    val = f64(wv).T @ x + f64(bv)
    future = np.triu(np.ones((T, T), bool), 1)
    o = np.zeros((E, N))
    for b in range(B):
        cols = slice(b * T, (b + 1) * T)
        for h in range(H):
            rows = slice(h * D, (h + 1) * D)
            score = qry[rows, cols].T @ key[rows, cols] / np.sqrt(D)
            score = np.where(future, -1e9, score)
            e = np.exp(score - score.max(axis=1, keepdims=True))
            prob = e / e.sum(axis=1, keepdims=True)
            o[rows, cols] = val[rows, cols] @ prob.T
    attn = f64(wo).T @ o + f64(bo)
    return x + np.maximum(attn, 0.0)

@@ -1,0 +1,168 @@
+import math
+
+import concourse.mybir as mybir
+from concourse.masks import make_identity
+
+F32 = mybir.dt.float32
+BF16 = mybir.dt.bfloat16
+U16 = mybir.dt.uint16
+ADD = mybir.AluOpType.add
+MULT = mybir.AluOpType.mult
+IS_GE = mybir.AluOpType.is_ge
+ACT = mybir.ActivationFunctionType
+ALONG_FREE = mybir.AxisListType.X
+
+P = 128
+E, V, B, T, H, D = 512, 512, 4, 512, 4, 128
+N = B * T
+EB = E // P
+TB = T // P
+SCALE = 1.0 / math.sqrt(D)
+MASKED = -1.0e9
+
+FLOPS = 8 * E * E * N + 2 * B * H * D * T * (T + 1)
+
+
+def block(i):
+    return slice(i * P, (i + 1) * P)
+
+
+def tile_sakt_b_kernel(tc, table, pos, wq, bq, wk, wv, bv, wo, bo, offs, out):
+    nc = tc.nc
+    with (
+        tc.tile_pool(name="held", bufs=1) as held,
+        tc.tile_pool(name="sequence", bufs=2) as sequence,
+        tc.tile_pool(name="head", bufs=4) as head,
+        tc.tile_pool(name="work", bufs=3) as work,
+        tc.tile_pool(name="stat", bufs=6) as stat,
+        tc.psum_pool(name="acc_pool", bufs=2) as acc_pool,
+        tc.psum_pool(name="score_pool", bufs=3) as score_pool,
+        tc.psum_pool(name="flip_pool", bufs=2) as flip_pool,
+        tc.psum_pool(name="mix_pool", bufs=1) as mix_pool,
+    ):
+        offsets = held.tile([P, N // 16], U16, name="offsets")
+        nc.sync.dma_start(offsets[:], offs)
+
+        def load_weight(w, name):
+            w_sb = held.tile([P, EB, E], BF16, name=name)
+            nc.scalar.dma_start(w_sb[:], w.rearrange("(a p) m -> p a m", p=P))
+            return w_sb
+
+        def load_bias(b, name):
+            b_sb = held.tile([P, EB], F32, name=name)
+            with nc.allow_non_contiguous_dma(reason="512 single values, once"):
+                nc.scalar.dma_start(b_sb[:], b.rearrange("(a p) o -> p (a o)", p=P))
+            return b_sb
+
+        wv_sb = load_weight(wv, "wv_sb")
+        wq_sb = load_weight(wq, "wq_sb")
+        wk_sb = load_weight(wk, "wk_sb")
+        bq_sb = load_bias(bq, "bq_sb")
+        bv_sb = load_bias(bv, "bv_sb")
+        bo_sb = load_bias(bo, "bo_sb")
+        wo_sb = load_weight(wo, "wo_sb")
+
+        table_sb = [held.tile([P, V], F32, name=f"table{c}") for c in range(EB)]
+        pos_sb = [[held.tile([P, T], F32, name=f"pos{b}_{c}") for c in range(EB)] for b in range(B)]
+        for c in range(EB):
+            nc.sync.dma_start(table_sb[c][:], table[block(c), :])
+            nc.sync.dma_start(pos_sb[0][c][:], pos[block(c), 0:T])
+        for b in range(1, B):
+            for c in range(EB):
+                nc.sync.dma_start(pos_sb[b][c][:], pos[block(c), b * T : (b + 1) * T])
+
+        ident = held.tile([P, P], BF16, name="ident")
+        make_identity(nc, ident[:])
+        future = held.tile([P, P], BF16, name="future")
+        nc.gpsimd.memset(future[:], 0.0)
+        nc.gpsimd.affine_select(
+            out=future[:], in_=future[:], pattern=[[-1, P]], compare_op=IS_GE,
+            fill=MASKED, base=0, channel_multiplier=1,
+        )
+        bq_scaled = held.tile([P, H], F32, name="bq_scaled")
+        nc.vector.tensor_scalar(bq_scaled[:], bq_sb[:], SCALE, None, MULT)
+
+        def embed(b):
+            x = [held.tile([P, T], F32, name=f"x{b}_{c}") for c in range(EB)]
+            x_bf = sequence.tile([P, EB, T], BF16, name="x_bf")
+            for c in range(EB):
+                picked = table_sb[c][:].indirect(offsets[:, b * (T // 16) : (b + 1) * (T // 16)])
+                nc.vector.tensor_tensor(x[c][:], picked, pos_sb[b][c][:], ADD)
+                nc.scalar.copy(x_bf[:, c, :], x[c][:])
+            return x, x_bf
+
+        def values(x_bf):
+            val_t = sequence.tile([P, TB, E], BF16, name="val_t")
+            for i in range(TB):
+                acc = acc_pool.tile([P, E], F32, name="acc")
+                for c in range(EB):
+                    nc.tensor.matmul(acc[:], lhsT=x_bf[:, c, block(i)], rhs=wv_sb[:, c, :],
+                                     start=(c == 0), stop=(c == EB - 1))
+                nc.scalar.copy(val_t[:, i, :], acc[:])
+            return val_t
+
+        def project(w_sb, h, x_bf):
+            acc = acc_pool.tile([P, T], F32, name="acc")
+            for c in range(EB):
+                nc.tensor.matmul(acc[:], lhsT=w_sb[:, c, block(h)], rhs=x_bf[:, c, :],
+                                 start=(c == 0), stop=(c == EB - 1))
+            return acc
+
+        def attend(h, x_bf, val_t, o_bf):
+            qry = head.tile([P, T], BF16, name="qry")
+            nc.scalar.activation(qry[:], project(wq_sb, h, x_bf)[:], ACT.Identity,
+                                 bias=bq_scaled[:, h : h + 1], scale=SCALE)
+            key = head.tile([P, T], BF16, name="key")
+            nc.vector.tensor_copy(key[:], project(wk_sb, h, x_bf)[:])
+
+            mixed = mix_pool.tile([P, T], F32, name="mixed")
+            for t in range(TB):
+                seen = (t + 1) * P
+                score = score_pool.tile([P, T], F32, name="score")
+                nc.tensor.matmul(score[:, :seen], lhsT=qry[:, block(t)], rhs=key[:, :seen],
+                                 start=True, stop=False)
+                nc.tensor.matmul(score[:, block(t)], lhsT=ident[:], rhs=future[:],
+                                 start=False, stop=True)
+
+                neg_max = stat.tile([P, 1], F32, name="neg_max")
+                nc.vector.reduce_max(neg_max[:], score[:, :seen], axis=ALONG_FREE, negate=True)
+                weight = work.tile([P, T], BF16, name="weight")
+                total = stat.tile([P, 1], F32, name="total")
+                nc.scalar.activation(weight[:, :seen], score[:, :seen], ACT.Exp,
+                                     bias=neg_max[:], scale=1.0, accum_out=total[:])
+
+                share = stat.tile([P, 1], F32, name="share")
+                nc.vector.reciprocal(share[:], total[:])
+                divider = work.tile([P, P], BF16, name="divider")
+                nc.vector.tensor_scalar(divider[:], ident[:], share[:], None, MULT)
+                flipped = flip_pool.tile([P, T], BF16, name="flipped")
+                for i in range(t + 1):
+                    nc.tensor.matmul(flipped[:, block(i)], lhsT=weight[:, block(i)], rhs=divider[:],
+                                     start=True, stop=True)
+                prob_t = work.tile([P, T], BF16, name="prob_t")
+                nc.vector.tensor_copy(prob_t[:, :seen], flipped[:, :seen])
+
+                for i in range(t + 1):
+                    nc.tensor.matmul(mixed[:, block(t)], lhsT=val_t[:, i, block(h)],
+                                     rhs=prob_t[:, block(i)], start=(i == 0), stop=(i == t))
+            nc.vector.tensor_scalar(o_bf[:, h, :], mixed[:], bv_sb[:, h : h + 1], None, ADD)
+
+        def finish(b, x, o_bf):
+            for a in range(EB):
+                acc = acc_pool.tile([P, T], F32, name="acc")
+                for h in range(H):
+                    nc.tensor.matmul(acc[:], lhsT=wo_sb[:, h, block(a)], rhs=o_bf[:, h, :],
+                                     start=(h == 0), stop=(h == H - 1))
+                gain = work.tile([P, T], F32, name="gain")
+                nc.scalar.activation(gain[:], acc[:], ACT.Relu, bias=bo_sb[:, a : a + 1], scale=1.0)
+                y = work.tile([P, T], F32, name="y")
+                nc.gpsimd.tensor_tensor(y[:], gain[:], x[a][:], ADD)
+                nc.sync.dma_start(out[block(a), b * T : (b + 1) * T], y[:])
+
+        for b in range(B):
+            x, x_bf = embed(b)
+            val_t = values(x_bf)
+            o_bf = sequence.tile([P, H, T], BF16, name="o_bf")
+            for h in range(H):
+                attend(h, x_bf, val_t, o_bf)
+            finish(b, x, o_bf)

@@ -31,12 +31,11 @@ def tile_sakt_b_kernel(tc, table, pos, wq, bq, wk, wv, bv, wo, bo, offs, out):
     nc = tc.nc
     with (
         tc.tile_pool(name="held", bufs=1) as held,
-        tc.tile_pool(name="sequence", bufs=2) as sequence,
-        tc.tile_pool(name="head", bufs=4) as head,
-        tc.tile_pool(name="work", bufs=3) as work,
+        tc.tile_pool(name="sequence", bufs=3) as sequence,
+        tc.tile_pool(name="head", bufs=3) as head,
+        tc.tile_pool(name="work", bufs=6) as work,
         tc.tile_pool(name="stat", bufs=6) as stat,
-        tc.psum_pool(name="acc_pool", bufs=2) as acc_pool,
-        tc.psum_pool(name="score_pool", bufs=3) as score_pool,
+        tc.psum_pool(name="sum_pool", bufs=5) as sum_pool,
         tc.psum_pool(name="flip_pool", bufs=2) as flip_pool,
         tc.psum_pool(name="mix_pool", bufs=1) as mix_pool,
     ):
@@ -45,7 +44,7 @@ def tile_sakt_b_kernel(tc, table, pos, wq, bq, wk, wv, bv, wo, bo, offs, out):
 
         def load_weight(w, name):
             w_sb = held.tile([P, EB, E], BF16, name=name)
-            nc.scalar.dma_start(w_sb[:], w.rearrange("(a p) m -> p a m", p=P))
+            nc.sync.dma_start(w_sb[:], w.rearrange("(a p) m -> p a m", p=P))
             return w_sb
 
         def load_bias(b, name):
@@ -54,22 +53,26 @@ def tile_sakt_b_kernel(tc, table, pos, wq, bq, wk, wv, bv, wo, bo, offs, out):
                 nc.scalar.dma_start(b_sb[:], b.rearrange("(a p) o -> p (a o)", p=P))
             return b_sb
 
-        wv_sb = load_weight(wv, "wv_sb")
-        wq_sb = load_weight(wq, "wq_sb")
-        wk_sb = load_weight(wk, "wk_sb")
+        def load_pos(b, c):
+            nc.sync.dma_start(pos_sb[b][c][:], pos[block(c), b * T : (b + 1) * T])
+
         bq_sb = load_bias(bq, "bq_sb")
         bv_sb = load_bias(bv, "bv_sb")
         bo_sb = load_bias(bo, "bo_sb")
-        wo_sb = load_weight(wo, "wo_sb")
-
+        wv_sb = load_weight(wv, "wv_sb")
         table_sb = [held.tile([P, V], F32, name=f"table{c}") for c in range(EB)]
         pos_sb = [[held.tile([P, T], F32, name=f"pos{b}_{c}") for c in range(EB)] for b in range(B)]
         for c in range(EB):
             nc.sync.dma_start(table_sb[c][:], table[block(c), :])
-            nc.sync.dma_start(pos_sb[0][c][:], pos[block(c), 0:T])
-        for b in range(1, B):
+            load_pos(0, c)
+        wq_sb = load_weight(wq, "wq_sb")
+        wk_sb = load_weight(wk, "wk_sb")
+        for c in range(EB):
+            load_pos(1, c)
+        wo_sb = load_weight(wo, "wo_sb")
+        for b in range(2, B):
             for c in range(EB):
-                nc.sync.dma_start(pos_sb[b][c][:], pos[block(c), b * T : (b + 1) * T])
+                load_pos(b, c)
 
         ident = held.tile([P, P], BF16, name="ident")
         make_identity(nc, ident[:])
@@ -82,87 +85,135 @@ def tile_sakt_b_kernel(tc, table, pos, wq, bq, wk, wv, bv, wo, bo, offs, out):
         bq_scaled = held.tile([P, H], F32, name="bq_scaled")
         nc.vector.tensor_scalar(bq_scaled[:], bq_sb[:], SCALE, None, MULT)
 
-        def embed(b):
-            x = [held.tile([P, T], F32, name=f"x{b}_{c}") for c in range(EB)]
-            x_bf = sequence.tile([P, EB, T], BF16, name="x_bf")
-            for c in range(EB):
-                picked = table_sb[c][:].indirect(offsets[:, b * (T // 16) : (b + 1) * (T // 16)])
-                nc.vector.tensor_tensor(x[c][:], picked, pos_sb[b][c][:], ADD)
-                nc.scalar.copy(x_bf[:, c, :], x[c][:])
-            return x, x_bf
+        x = [[held.tile([P, T], F32, name=f"x{b}_{c}") for c in range(EB)] for b in range(B)]
+        x_bf = [held.tile([P, EB, T], BF16, name=f"x_bf{b}") for b in range(B)]
+        val_t = {}
+        o_bf = {}
+        qry = {}
+        key = {}
 
-        def values(x_bf):
-            val_t = sequence.tile([P, TB, E], BF16, name="val_t")
-            for i in range(TB):
-                acc = acc_pool.tile([P, E], F32, name="acc")
-                for c in range(EB):
-                    nc.tensor.matmul(acc[:], lhsT=x_bf[:, c, block(i)], rhs=wv_sb[:, c, :],
-                                     start=(c == 0), stop=(c == EB - 1))
-                nc.scalar.copy(val_t[:, i, :], acc[:])
-            return val_t
+        def embed(b, c):
+            picked = table_sb[c][:].indirect(offsets[:, b * (T // 16) : (b + 1) * (T // 16)])
+            nc.vector.tensor_tensor(x[b][c][:], picked, pos_sb[b][c][:], ADD)
+            nc.scalar.copy(x_bf[b][:, c, :], x[b][c][:])
 
-        def project(w_sb, h, x_bf):
-            acc = acc_pool.tile([P, T], F32, name="acc")
+        def values(b, i):
+            if i == 0:
+                val_t[b] = sequence.tile([P, TB, E], BF16, name="val_t")
+            acc = sum_pool.tile([P, E], F32, name="acc", tag="sum")
             for c in range(EB):
-                nc.tensor.matmul(acc[:], lhsT=w_sb[:, c, block(h)], rhs=x_bf[:, c, :],
+                nc.tensor.matmul(acc[:], lhsT=x_bf[b][:, c, block(i)], rhs=wv_sb[:, c, :],
+                                 start=(c == 0), stop=(c == EB - 1))
+            nc.scalar.copy(val_t[b][:, i, :], acc[:])
+
+        def project(w_sb, n):
+            b, h = divmod(n, H)
+            acc = sum_pool.tile([P, T], F32, name="acc", tag="sum")
+            for c in range(EB):
+                nc.tensor.matmul(acc[:], lhsT=w_sb[:, c, block(h)], rhs=x_bf[b][:, c, :],
                                  start=(c == 0), stop=(c == EB - 1))
             return acc
 
-        def attend(h, x_bf, val_t, o_bf):
-            qry = head.tile([P, T], BF16, name="qry")
-            nc.scalar.activation(qry[:], project(wq_sb, h, x_bf)[:], ACT.Identity,
-                                 bias=bq_scaled[:, h : h + 1], scale=SCALE)
-            key = head.tile([P, T], BF16, name="key")
-            nc.vector.tensor_copy(key[:], project(wk_sb, h, x_bf)[:])
+        def queries(n):
+            qry[n] = head.tile([P, T], BF16, name="qry")
+            nc.scalar.activation(qry[n][:], project(wq_sb, n)[:], ACT.Identity,
+                                 bias=bq_scaled[:, n % H : n % H + 1], scale=SCALE)
 
-            mixed = mix_pool.tile([P, T], F32, name="mixed")
-            for t in range(TB):
-                seen = (t + 1) * P
-                score = score_pool.tile([P, T], F32, name="score")
-                nc.tensor.matmul(score[:, :seen], lhsT=qry[:, block(t)], rhs=key[:, :seen],
-                                 start=True, stop=False)
-                nc.tensor.matmul(score[:, block(t)], lhsT=ident[:], rhs=future[:],
-                                 start=False, stop=True)
+        def keys(n):
+            key[n] = head.tile([P, T], BF16, name="key")
+            nc.scalar.copy(key[n][:], project(wk_sb, n)[:])
 
-                neg_max = stat.tile([P, 1], F32, name="neg_max")
-                nc.vector.reduce_max(neg_max[:], score[:, :seen], axis=ALONG_FREE, negate=True)
-                weight = work.tile([P, T], BF16, name="weight")
-                total = stat.tile([P, 1], F32, name="total")
-                nc.scalar.activation(weight[:, :seen], score[:, :seen], ACT.Exp,
-                                     bias=neg_max[:], scale=1.0, accum_out=total[:])
-
-                share = stat.tile([P, 1], F32, name="share")
-                nc.vector.reciprocal(share[:], total[:])
-                divider = work.tile([P, P], BF16, name="divider")
-                nc.vector.tensor_scalar(divider[:], ident[:], share[:], None, MULT)
-                flipped = flip_pool.tile([P, T], BF16, name="flipped")
-                for i in range(t + 1):
-                    nc.tensor.matmul(flipped[:, block(i)], lhsT=weight[:, block(i)], rhs=divider[:],
-                                     start=True, stop=True)
-                prob_t = work.tile([P, T], BF16, name="prob_t")
-                nc.vector.tensor_copy(prob_t[:, :seen], flipped[:, :seen])
-
-                for i in range(t + 1):
-                    nc.tensor.matmul(mixed[:, block(t)], lhsT=val_t[:, i, block(h)],
-                                     rhs=prob_t[:, block(i)], start=(i == 0), stop=(i == t))
-            nc.vector.tensor_scalar(o_bf[:, h, :], mixed[:], bv_sb[:, h : h + 1], None, ADD)
-
-        def finish(b, x, o_bf):
-            for a in range(EB):
-                acc = acc_pool.tile([P, T], F32, name="acc")
-                for h in range(H):
-                    nc.tensor.matmul(acc[:], lhsT=wo_sb[:, h, block(a)], rhs=o_bf[:, h, :],
-                                     start=(h == 0), stop=(h == H - 1))
-                gain = work.tile([P, T], F32, name="gain")
-                nc.scalar.activation(gain[:], acc[:], ACT.Relu, bias=bo_sb[:, a : a + 1], scale=1.0)
-                y = work.tile([P, T], F32, name="y")
-                nc.gpsimd.tensor_tensor(y[:], gain[:], x[a][:], ADD)
-                nc.sync.dma_start(out[block(a), b * T : (b + 1) * T], y[:])
-
-        for b in range(B):
-            x, x_bf = embed(b)
-            val_t = values(x_bf)
-            o_bf = sequence.tile([P, H, T], BF16, name="o_bf")
+        def finish(b, a):
+            acc = sum_pool.tile([P, T], F32, name="acc", tag="sum")
             for h in range(H):
-                attend(h, x_bf, val_t, o_bf)
-            finish(b, x, o_bf)
+                nc.tensor.matmul(acc[:], lhsT=wo_sb[:, h, block(a)], rhs=o_bf[b][:, h, :],
+                                 start=(h == 0), stop=(h == H - 1))
+            gain = work.tile([P, T], F32, name="gain")
+            nc.scalar.activation(gain[:], acc[:], ACT.Relu, bias=bo_sb[:, a : a + 1], scale=1.0)
+            y = work.tile([P, T], F32, name="y")
+            nc.vector.tensor_tensor(y[:], gain[:], x[b][a][:], ADD)
+            nc.sync.dma_start(out[block(a), b * T : (b + 1) * T], y[:])
+
+        weight = {}
+        total = {}
+        divider = {}
+        prob_t = {}
+        mixed = {}
+
+        def weigh(n, t):
+            seen = (t + 1) * P
+            score = sum_pool.tile([P, T], F32, name="score", tag="sum")
+            nc.tensor.matmul(score[:, :seen], lhsT=qry[n][:, block(t)], rhs=key[n][:, :seen],
+                             start=True, stop=False)
+            nc.tensor.matmul(score[:, block(t)], lhsT=ident[:], rhs=future[:], start=False, stop=True)
+            neg_max = stat.tile([P, 1], F32, name="neg_max")
+            nc.vector.reduce_max(neg_max[:], score[:, :seen], axis=ALONG_FREE, negate=True)
+            weight[n, t] = work.tile([P, T], BF16, name="weight")
+            total[n, t] = stat.tile([P, 1], F32, name="total")
+            nc.scalar.activation(weight[n, t][:, :seen], score[:, :seen], ACT.Exp,
+                                 bias=neg_max[:], scale=1.0, accum_out=total[n, t][:])
+
+        def divide(n, t):
+            share = stat.tile([P, 1], F32, name="share")
+            nc.vector.reciprocal(share[:], total[n, t][:])
+            divider[n, t] = work.tile([P, P], BF16, name="divider")
+            nc.vector.tensor_scalar(divider[n, t][:], ident[:], share[:], None, MULT)
+
+        def flip(n, t):
+            seen = (t + 1) * P
+            flipped = flip_pool.tile([P, T], BF16, name="flipped")
+            for i in range(t + 1):
+                nc.tensor.matmul(flipped[:, block(i)], lhsT=weight[n, t][:, block(i)],
+                                 rhs=divider[n, t][:], start=True, stop=True)
+            prob_t[n, t] = work.tile([P, T], BF16, name="prob_t")
+            nc.vector.tensor_copy(prob_t[n, t][:, :seen], flipped[:, :seen])
+
+        def mix(n, t):
+            b, h = divmod(n, H)
+            if t == TB - 1:
+                mixed[n] = mix_pool.tile([P, T], F32, name="mixed")
+            for i in range(t + 1):
+                nc.tensor.matmul(mixed[n][:, block(t)], lhsT=val_t[b][:, i, block(h)],
+                                 rhs=prob_t[n, t][:, block(i)], start=(i == 0), stop=(i == t))
+            if t == 0:
+                if h == 0:
+                    o_bf[b] = sequence.tile([P, H, T], BF16, name="o_bf")
+                nc.vector.tensor_scalar(o_bf[b][:, h, :], mixed[n][:], bv_sb[:, h : h + 1], None, ADD)
+
+        def fill(n, t):
+            b, h = divmod(n, H)
+            if t == 3 and n + 1 < B * H:
+                queries(n + 1)
+            if t == 2 and n + 1 < B * H:
+                keys(n + 1)
+            if t == 1 and b + 1 < B:
+                values(b + 1, h)
+            if t == 0 and n >= H + 1:
+                finish(*divmod(n - H - 1, EB))
+            if t == 3 and b + 2 < B:
+                embed(b + 2, h)
+
+        for c in range(EB):
+            embed(0, c)
+        for i in range(TB):
+            values(0, i)
+        queries(0)
+        keys(0)
+        for c in range(EB):
+            embed(1, c)
+
+        blocks = [(n, t) for n in range(B * H) for t in reversed(range(TB))]
+        for s in range(len(blocks) + 4):
+            if s < len(blocks):
+                weigh(*blocks[s])
+            if 2 <= s < len(blocks) + 2:
+                divide(*blocks[s - 2])
+            if 3 <= s < len(blocks) + 3:
+                flip(*blocks[s - 3])
+            if 4 <= s:
+                mix(*blocks[s - 4])
+            if s < len(blocks):
+                fill(*blocks[s])
+
+        for m in range(B * H - H - 1, B * EB):
+            finish(*divmod(m, EB))

@@ -74,6 +74,10 @@ def tile_sakt_b_kernel(tc, table, pos, wq, bq, wk, wv, bv, wo, bo, offs, out):
             for c in range(EB):
                 load_pos(b, c)
 
+        warm = held.tile([P, 1], F32, name="warm")
+        nc.vector.memset(warm[:], 0.0)
+        nc.scalar.activation(warm[:], warm[:], ACT.Exp)
+
         ident = held.tile([P, P], BF16, name="ident")
         make_identity(nc, ident[:])
         future = held.tile([P, P], BF16, name="future")

@@ -47,18 +47,15 @@ def tile_sakt_b_kernel(tc, table, pos, wq, bq, wk, wv, bv, wo, bo, offs, out):
             nc.sync.dma_start(w_sb[:], w.rearrange("(a p) m -> p a m", p=P))
             return w_sb
 
-        def load_bias(b, name):
-            b_sb = held.tile([P, EB], F32, name=name)
+        def load_bias(bias, name):
+            bias_sb = held.tile([P, EB], F32, name=name)
             with nc.allow_non_contiguous_dma(reason="512 single values, once"):
-                nc.scalar.dma_start(b_sb[:], b.rearrange("(a p) o -> p (a o)", p=P))
-            return b_sb
+                nc.sync.dma_start(bias_sb[:], bias.rearrange("(a p) o -> p (a o)", p=P))
+            return bias_sb
 
         def load_pos(b, c):
             nc.sync.dma_start(pos_sb[b][c][:], pos[block(c), b * T : (b + 1) * T])
 
-        bq_sb = load_bias(bq, "bq_sb")
-        bv_sb = load_bias(bv, "bv_sb")
-        bo_sb = load_bias(bo, "bo_sb")
         wv_sb = load_weight(wv, "wv_sb")
         table_sb = [held.tile([P, V], F32, name=f"table{c}") for c in range(EB)]
         pos_sb = [[held.tile([P, T], F32, name=f"pos{b}_{c}") for c in range(EB)] for b in range(B)]
@@ -67,16 +64,15 @@ def tile_sakt_b_kernel(tc, table, pos, wq, bq, wk, wv, bv, wo, bo, offs, out):
             load_pos(0, c)
         wq_sb = load_weight(wq, "wq_sb")
         wk_sb = load_weight(wk, "wk_sb")
+        bq_sb = load_bias(bq, "bq_sb")
         for c in range(EB):
             load_pos(1, c)
+        bv_sb = load_bias(bv, "bv_sb")
         wo_sb = load_weight(wo, "wo_sb")
+        bo_sb = load_bias(bo, "bo_sb")
         for b in range(2, B):
             for c in range(EB):
                 load_pos(b, c)
-
-        warm = held.tile([P, 1], F32, name="warm")
-        nc.vector.memset(warm[:], 0.0)
-        nc.scalar.activation(warm[:], warm[:], ACT.Exp)
 
         ident = held.tile([P, P], BF16, name="ident")
         make_identity(nc, ident[:])
@@ -186,15 +182,16 @@ def tile_sakt_b_kernel(tc, table, pos, wq, bq, wk, wv, bv, wo, bo, offs, out):
 
         def fill(n, t):
             b, h = divmod(n, H)
-            if t == 3 and n + 1 < B * H:
+            turn = TB - 1 - t
+            if turn == 0 and n + 1 < B * H:
                 queries(n + 1)
-            if t == 2 and n + 1 < B * H:
+            if turn == 1 and n + 1 < B * H:
                 keys(n + 1)
-            if t == 1 and b + 1 < B:
+            if turn == 2 and b + 1 < B:
                 values(b + 1, h)
-            if t == 0 and n >= H + 1:
+            if turn == 3 and n >= H + 1:
                 finish(*divmod(n - H - 1, EB))
-            if t == 3 and b + 2 < B:
+            if turn == 0 and b + 2 < B:
                 embed(b + 2, h)
 
         for c in range(EB):
@@ -206,18 +203,18 @@ def tile_sakt_b_kernel(tc, table, pos, wq, bq, wk, wv, bv, wo, bo, offs, out):
         for c in range(EB):
             embed(1, c)
 
-        blocks = [(n, t) for n in range(B * H) for t in reversed(range(TB))]
-        for s in range(len(blocks) + 4):
-            if s < len(blocks):
-                weigh(*blocks[s])
-            if 2 <= s < len(blocks) + 2:
-                divide(*blocks[s - 2])
-            if 3 <= s < len(blocks) + 3:
-                flip(*blocks[s - 3])
+        query_blocks = [(n, t) for n in range(B * H) for t in reversed(range(TB))]
+        for s in range(len(query_blocks) + 4):
+            if s < len(query_blocks):
+                weigh(*query_blocks[s])
+            if 2 <= s < len(query_blocks) + 2:
+                divide(*query_blocks[s - 2])
+            if 3 <= s < len(query_blocks) + 3:
+                flip(*query_blocks[s - 3])
             if 4 <= s:
-                mix(*blocks[s - 4])
-            if s < len(blocks):
-                fill(*blocks[s])
+                mix(*query_blocks[s - 4])
+            if s < len(query_blocks):
+                fill(*query_blocks[s])
 
         for m in range(B * H - H - 1, B * EB):
             finish(*divmod(m, EB))

@@ -136,7 +136,7 @@ def tile_sakt_b_kernel(tc, table, pos, wq, bq, wk, wv, bv, wo, bo, offs, out):
 
         weight = {}
         total = {}
-        divider = {}
+        prob = {}
         prob_t = {}
         mixed = {}
 
@@ -154,17 +154,17 @@ def tile_sakt_b_kernel(tc, table, pos, wq, bq, wk, wv, bv, wo, bo, offs, out):
                                  bias=neg_max[:], scale=1.0, accum_out=total[n, t][:])
 
         def divide(n, t):
+            seen = (t + 1) * P
             share = stat.tile([P, 1], F32, name="share")
             nc.vector.reciprocal(share[:], total[n, t][:])
-            divider[n, t] = work.tile([P, P], BF16, name="divider")
-            nc.vector.tensor_scalar(divider[n, t][:], ident[:], share[:], None, MULT)
+            prob[n, t] = work.tile([P, T], BF16, name="prob")
+            nc.vector.tensor_scalar(prob[n, t][:, :seen], weight[n, t][:, :seen], share[:], None, MULT)
 
         def flip(n, t):
             seen = (t + 1) * P
             flipped = flip_pool.tile([P, T], BF16, name="flipped")
             for i in range(t + 1):
-                nc.tensor.matmul(flipped[:, block(i)], lhsT=weight[n, t][:, block(i)],
-                                 rhs=divider[n, t][:], start=True, stop=True)
+                nc.tensor.transpose(flipped[:, block(i)], prob[n, t][:, block(i)], ident[:])
             prob_t[n, t] = work.tile([P, T], BF16, name="prob_t")
             nc.vector.tensor_copy(prob_t[n, t][:, :seen], flipped[:, :seen])
 

@@ -204,16 +204,18 @@ def tile_sakt_b_kernel(tc, table, pos, wq, bq, wk, wv, bv, wo, bo, offs, out):
             embed(1, c)
 
         query_blocks = [(n, t) for n in range(B * H) for t in reversed(range(TB))]
-        for s in range(len(query_blocks) + 4):
-            if s < len(query_blocks):
+        DIVIDE_AFTER, FLIP_AFTER, MIX_AFTER = 2, 4, 6
+        blocks = len(query_blocks)
+        for s in range(blocks + MIX_AFTER):
+            if s < blocks:
                 weigh(*query_blocks[s])
-            if 2 <= s < len(query_blocks) + 2:
-                divide(*query_blocks[s - 2])
-            if 3 <= s < len(query_blocks) + 3:
-                flip(*query_blocks[s - 3])
-            if 4 <= s:
-                mix(*query_blocks[s - 4])
-            if s < len(query_blocks):
+            if 0 <= s - DIVIDE_AFTER < blocks:
+                divide(*query_blocks[s - DIVIDE_AFTER])
+            if 0 <= s - FLIP_AFTER < blocks:
+                flip(*query_blocks[s - FLIP_AFTER])
+            if 0 <= s - MIX_AFTER:
+                mix(*query_blocks[s - MIX_AFTER])
+            if s < blocks:
                 fill(*query_blocks[s])
 
         for m in range(B * H - H - 1, B * EB):

@@ -32,7 +32,6 @@ def tile_sakt_b_kernel(tc, table, pos, wq, bq, wk, wv, bv, wo, bo, offs, out):
     with (
         tc.tile_pool(name="held", bufs=1) as held,
         tc.tile_pool(name="sequence", bufs=3) as sequence,
-        tc.tile_pool(name="head", bufs=3) as head,
         tc.tile_pool(name="work", bufs=6) as work,
         tc.tile_pool(name="stat", bufs=6) as stat,
         tc.psum_pool(name="sum_pool", bufs=5) as sum_pool,
@@ -53,18 +52,20 @@ def tile_sakt_b_kernel(tc, table, pos, wq, bq, wk, wv, bv, wo, bo, offs, out):
                 nc.sync.dma_start(bias_sb[:], bias.rearrange("(a p) o -> p (a o)", p=P))
             return bias_sb
 
+        table_sb = [held.tile([P, V], F32, name=f"table{c}") for c in range(EB)]
+        pos_sb = [[held.tile([P, T], F32, name=f"pos{b}_{c}") for c in range(EB)] for b in range(B)]
+
         def load_pos(b, c):
             nc.sync.dma_start(pos_sb[b][c][:], pos[block(c), b * T : (b + 1) * T])
 
-        wv_sb = load_weight(wv, "wv_sb")
-        table_sb = [held.tile([P, V], F32, name=f"table{c}") for c in range(EB)]
-        pos_sb = [[held.tile([P, T], F32, name=f"pos{b}_{c}") for c in range(EB)] for b in range(B)]
         for c in range(EB):
             nc.sync.dma_start(table_sb[c][:], table[block(c), :])
             load_pos(0, c)
+            if c == 1:
+                wv_sb = load_weight(wv, "wv_sb")
+        bq_sb = load_bias(bq, "bq_sb")
         wq_sb = load_weight(wq, "wq_sb")
         wk_sb = load_weight(wk, "wk_sb")
-        bq_sb = load_bias(bq, "bq_sb")
         for c in range(EB):
             load_pos(1, c)
         bv_sb = load_bias(bv, "bv_sb")
@@ -82,29 +83,35 @@ def tile_sakt_b_kernel(tc, table, pos, wq, bq, wk, wv, bv, wo, bo, offs, out):
             out=future[:], in_=future[:], pattern=[[-1, P]], compare_op=IS_GE,
             fill=MASKED, base=0, channel_multiplier=1,
         )
-        bq_scaled = held.tile([P, H], F32, name="bq_scaled")
-        nc.vector.tensor_scalar(bq_scaled[:], bq_sb[:], SCALE, None, MULT)
 
         x = [[held.tile([P, T], F32, name=f"x{b}_{c}") for c in range(EB)] for b in range(B)]
         x_bf = [held.tile([P, EB, T], BF16, name=f"x_bf{b}") for b in range(B)]
+        o_bf = [held.tile([P, H, T], BF16, name=f"o_bf{b}") for b in range(B)]
         val_t = {}
-        o_bf = {}
         qry = {}
         key = {}
+        val_sum = {}
 
-        def embed(b, c):
+        def look_up(b, c):
             picked = table_sb[c][:].indirect(offsets[:, b * (T // 16) : (b + 1) * (T // 16)])
             nc.vector.tensor_tensor(x[b][c][:], picked, pos_sb[b][c][:], ADD)
+
+        def round_x(b, c):
             nc.scalar.copy(x_bf[b][:, c, :], x[b][c][:])
+
+        def values_part(b, i, c):
+            if c == 0:
+                val_sum[b, i] = sum_pool.tile([P, E], F32, name="acc", tag="sum")
+            nc.tensor.matmul(val_sum[b, i][:], lhsT=x_bf[b][:, c, block(i)], rhs=wv_sb[:, c, :],
+                             start=(c == 0), stop=(c == EB - 1))
+            if c == EB - 1:
+                nc.scalar.copy(val_t[b][:, i, :], val_sum[b, i][:])
 
         def values(b, i):
             if i == 0:
                 val_t[b] = sequence.tile([P, TB, E], BF16, name="val_t")
-            acc = sum_pool.tile([P, E], F32, name="acc", tag="sum")
             for c in range(EB):
-                nc.tensor.matmul(acc[:], lhsT=x_bf[b][:, c, block(i)], rhs=wv_sb[:, c, :],
-                                 start=(c == 0), stop=(c == EB - 1))
-            nc.scalar.copy(val_t[b][:, i, :], acc[:])
+                values_part(b, i, c)
 
         def project(w_sb, n):
             b, h = divmod(n, H)
@@ -115,35 +122,47 @@ def tile_sakt_b_kernel(tc, table, pos, wq, bq, wk, wv, bv, wo, bo, offs, out):
             return acc
 
         def queries(n):
-            qry[n] = head.tile([P, T], BF16, name="qry")
-            nc.scalar.activation(qry[n][:], project(wq_sb, n)[:], ACT.Identity,
-                                 bias=bq_scaled[:, n % H : n % H + 1], scale=SCALE)
+            b, h = divmod(n, H)
+            if h == 0:
+                qry[b] = sequence.tile([P, H, T], BF16, name="qry")
+            nc.scalar.activation(qry[b][:, h, :], project(wq_sb, n)[:], ACT.Identity,
+                                 bias=bq_scaled[:, h : h + 1], scale=SCALE)
 
         def keys(n):
-            key[n] = head.tile([P, T], BF16, name="key")
-            nc.scalar.copy(key[n][:], project(wk_sb, n)[:])
+            b, h = divmod(n, H)
+            if h == 0:
+                key[b] = sequence.tile([P, H, T], BF16, name="key")
+            nc.scalar.copy(key[b][:, h, :], project(wk_sb, n)[:])
 
-        def finish(b, a):
-            acc = sum_pool.tile([P, T], F32, name="acc", tag="sum")
-            for h in range(H):
-                nc.tensor.matmul(acc[:], lhsT=wo_sb[:, h, block(a)], rhs=o_bf[b][:, h, :],
-                                 start=(h == 0), stop=(h == H - 1))
-            gain = work.tile([P, T], F32, name="gain")
-            nc.scalar.activation(gain[:], acc[:], ACT.Relu, bias=bo_sb[:, a : a + 1], scale=1.0)
-            y = work.tile([P, T], F32, name="y")
-            nc.vector.tensor_tensor(y[:], gain[:], x[b][a][:], ADD)
-            nc.sync.dma_start(out[block(a), b * T : (b + 1) * T], y[:])
+        def finish(b, tokens, feature_blocks):
+            width = tokens.stop - tokens.start
+            acc = {}
+            for a in feature_blocks:
+                acc[a] = sum_pool.tile([P, T], F32, name="acc", tag="sum")
+                for h in range(H - 1):
+                    nc.tensor.matmul(acc[a][:, :width], lhsT=wo_sb[:, h, block(a)], rhs=o_bf[b][:, h, tokens],
+                                     start=(h == 0), stop=False)
+            for a in feature_blocks:
+                nc.tensor.matmul(acc[a][:, :width], lhsT=wo_sb[:, H - 1, block(a)], rhs=o_bf[b][:, H - 1, tokens],
+                                 start=False, stop=True)
+                gain = work.tile([P, T], F32, name="gain")
+                nc.scalar.activation(gain[:, :width], acc[a][:, :width], ACT.Relu, bias=bo_sb[:, a : a + 1], scale=1.0)
+                y = work.tile([P, T], F32, name="y")
+                nc.vector.tensor_tensor(y[:, :width], gain[:, :width], x[b][a][:, tokens], ADD)
+                nc.sync.dma_start(out[block(a), b * T + tokens.start : b * T + tokens.stop], y[:, :width])
 
         weight = {}
         total = {}
         prob = {}
         prob_t = {}
         mixed = {}
+        LAST_HEAD = B * H - 1
 
         def weigh(n, t):
+            b, h = divmod(n, H)
             seen = (t + 1) * P
             score = sum_pool.tile([P, T], F32, name="score", tag="sum")
-            nc.tensor.matmul(score[:, :seen], lhsT=qry[n][:, block(t)], rhs=key[n][:, :seen],
+            nc.tensor.matmul(score[:, :seen], lhsT=qry[b][:, h, block(t)], rhs=key[b][:, h, :seen],
                              start=True, stop=False)
             nc.tensor.matmul(score[:, block(t)], lhsT=ident[:], rhs=future[:], start=False, stop=True)
             neg_max = stat.tile([P, 1], F32, name="neg_max")
@@ -175,48 +194,58 @@ def tile_sakt_b_kernel(tc, table, pos, wq, bq, wk, wv, bv, wo, bo, offs, out):
             for i in range(t + 1):
                 nc.tensor.matmul(mixed[n][:, block(t)], lhsT=val_t[b][:, i, block(h)],
                                  rhs=prob_t[n, t][:, block(i)], start=(i == 0), stop=(i == t))
-            if t == 0:
-                if h == 0:
-                    o_bf[b] = sequence.tile([P, H, T], BF16, name="o_bf")
-                nc.vector.tensor_scalar(o_bf[b][:, h, :], mixed[n][:], bv_sb[:, h : h + 1], None, ADD)
+            if n == LAST_HEAD:
+                done = block(t)
+            elif t == 0:
+                done = slice(0, T)
+            else:
+                return
+            nc.vector.tensor_scalar(o_bf[b][:, h, done], mixed[n][:, done], bv_sb[:, h : h + 1], None, ADD)
 
-        def fill(n, t):
+        def ride(n, t):
             b, h = divmod(n, H)
             turn = TB - 1 - t
-            if turn == 0 and n + 1 < B * H:
-                queries(n + 1)
-            if turn == 1 and n + 1 < B * H:
-                keys(n + 1)
-            if turn == 2 and b + 1 < B:
-                values(b + 1, h)
-            if turn == 3 and n >= H + 1:
-                finish(*divmod(n - H - 1, EB))
-            if turn == 0 and b + 2 < B:
-                embed(b + 2, h)
+            if b + 1 < B:
+                if turn == 0:
+                    queries(n + H)
+                if turn == 1:
+                    keys(n + H)
+                if turn == 2:
+                    values(b + 1, h)
+                if turn == 3 and b + 2 < B:
+                    look_up(b + 2, h)
+                    round_x(b + 2, h)
+            elif turn < 3:
+                earlier, a = divmod(3 * h + turn, EB)
+                finish(earlier, slice(0, T), [a])
 
+        val_t[0] = sequence.tile([P, TB, E], BF16, name="val_t")
         for c in range(EB):
-            embed(0, c)
-        for i in range(TB):
-            values(0, i)
-        queries(0)
-        keys(0)
-        for c in range(EB):
-            embed(1, c)
+            look_up(0, c)
+            round_x(0, c)
+            for i in range(TB):
+                values_part(0, i, c)
+        bq_scaled = held.tile([P, H], F32, name="bq_scaled")
+        nc.vector.tensor_scalar(bq_scaled[:], bq_sb[:], SCALE, None, MULT)
+        for h in range(H):
+            queries(h)
+            keys(h)
+            look_up(1, h)
+            round_x(1, h)
 
         query_blocks = [(n, t) for n in range(B * H) for t in reversed(range(TB))]
-        DIVIDE_AFTER, FLIP_AFTER, MIX_AFTER = 2, 4, 6
+        DIVIDE_AFTER, FLIP_AFTER, MIX_AFTER, FINISH_AFTER = 2, 4, 6, 7
         blocks = len(query_blocks)
-        for s in range(blocks + MIX_AFTER):
+        for s in range(blocks + FINISH_AFTER):
             if s < blocks:
                 weigh(*query_blocks[s])
             if 0 <= s - DIVIDE_AFTER < blocks:
                 divide(*query_blocks[s - DIVIDE_AFTER])
             if 0 <= s - FLIP_AFTER < blocks:
                 flip(*query_blocks[s - FLIP_AFTER])
-            if 0 <= s - MIX_AFTER:
+            if 0 <= s - MIX_AFTER < blocks:
                 mix(*query_blocks[s - MIX_AFTER])
             if s < blocks:
-                fill(*query_blocks[s])
-
-        for m in range(B * H - H - 1, B * EB):
-            finish(*divmod(m, EB))
+                ride(*query_blocks[s])
+            if s - FINISH_AFTER >= blocks - TB:
+                finish(B - 1, block(query_blocks[s - FINISH_AFTER][1]), range(EB))

@@ -200,7 +200,8 @@ def tile_sakt_b_kernel(tc, table, pos, wq, bq, wk, wv, bv, wo, bo, offs, out):
                 done = slice(0, T)
             else:
                 return
-            nc.vector.tensor_scalar(o_bf[b][:, h, done], mixed[n][:, done], bv_sb[:, h : h + 1], None, ADD)
+            nc.scalar.activation(o_bf[b][:, h, done], mixed[n][:, done], ACT.Identity,
+                                 bias=bv_sb[:, h : h + 1], scale=1.0)
 
         def ride(n, t):
             b, h = divmod(n, H)

@@ -177,7 +177,7 @@ def tile_sakt_b_kernel(tc, table, pos, wq, bq, wk, wv, bv, wo, bo, offs, out):
             share = stat.tile([P, 1], F32, name="share")
             nc.vector.reciprocal(share[:], total[n, t][:])
             prob[n, t] = work.tile([P, T], BF16, name="prob")
-            nc.vector.tensor_scalar(prob[n, t][:, :seen], weight[n, t][:, :seen], share[:], None, MULT)
+            nc.gpsimd.tensor_scalar(prob[n, t][:, :seen], weight[n, t][:, :seen], share[:], 1.0, MULT, MULT)
 
         def flip(n, t):
             seen = (t + 1) * P

@@ -34,9 +34,9 @@ def tile_sakt_b_kernel(tc, table, pos, wq, bq, wk, wv, bv, wo, bo, offs, out):
         tc.tile_pool(name="sequence", bufs=3) as sequence,
         tc.tile_pool(name="work", bufs=6) as work,
         tc.tile_pool(name="stat", bufs=6) as stat,
-        tc.psum_pool(name="sum_pool", bufs=5) as sum_pool,
+        tc.psum_pool(name="sum_pool", bufs=4) as sum_pool,
         tc.psum_pool(name="flip_pool", bufs=2) as flip_pool,
-        tc.psum_pool(name="mix_pool", bufs=1) as mix_pool,
+        tc.psum_pool(name="mix_pool", bufs=2) as mix_pool,
     ):
         offsets = held.tile([P, N // 16], U16, name="offsets")
         nc.sync.dma_start(offsets[:], offs)

@@ -151,6 +151,8 @@ def tile_sakt_b_kernel(tc, table, pos, wq, bq, wk, wv, bv, wo, bo, offs, out):
                 nc.vector.tensor_tensor(y[:, :width], gain[:, :width], x[b][a][:, tokens], ADD)
                 nc.sync.dma_start(out[block(a), b * T + tokens.start : b * T + tokens.stop], y[:, :width])
 
+        UNITS = [[3], [2], [1, 0]]
+        FIRST = {3: 0, 2: 0, 1: 0, 0: 2 * P}
         weight = {}
         total = {}
         prob = {}
@@ -158,66 +160,76 @@ def tile_sakt_b_kernel(tc, table, pos, wq, bq, wk, wv, bv, wo, bo, offs, out):
         mixed = {}
         LAST_HEAD = B * H - 1
 
-        def weigh(n, t):
+        def seen(t):
+            return slice(FIRST[t], FIRST[t] + (t + 1) * P)
+
+        def weigh(n, u):
             b, h = divmod(n, H)
-            seen = (t + 1) * P
             score = sum_pool.tile([P, T], F32, name="score", tag="sum")
-            nc.tensor.matmul(score[:, :seen], lhsT=qry[b][:, h, block(t)], rhs=key[b][:, h, :seen],
-                             start=True, stop=False)
-            nc.tensor.matmul(score[:, block(t)], lhsT=ident[:], rhs=future[:], start=False, stop=True)
-            neg_max = stat.tile([P, 1], F32, name="neg_max")
-            nc.vector.reduce_max(neg_max[:], score[:, :seen], axis=ALONG_FREE, negate=True)
-            weight[n, t] = work.tile([P, T], BF16, name="weight")
-            total[n, t] = stat.tile([P, 1], F32, name="total")
-            nc.scalar.activation(weight[n, t][:, :seen], score[:, :seen], ACT.Exp,
-                                 bias=neg_max[:], scale=1.0, accum_out=total[n, t][:])
+            for t in UNITS[u]:
+                nc.tensor.matmul(score[:, seen(t)], lhsT=qry[b][:, h, block(t)], rhs=key[b][:, h, : (t + 1) * P],
+                                 start=True, stop=False)
+                own = slice(seen(t).stop - P, seen(t).stop)
+                nc.tensor.matmul(score[:, own], lhsT=ident[:], rhs=future[:], start=False, stop=True)
+            neg_max = stat.tile([P, len(UNITS[u])], F32, name="neg_max")
+            weight[n, u] = work.tile([P, T], BF16, name="weight")
+            total[n, u] = stat.tile([P, len(UNITS[u])], F32, name="total")
+            for k, t in enumerate(UNITS[u]):
+                nc.vector.reduce_max(neg_max[:, k : k + 1], score[:, seen(t)], axis=ALONG_FREE, negate=True)
+                nc.scalar.activation(weight[n, u][:, seen(t)], score[:, seen(t)], ACT.Exp,
+                                     bias=neg_max[:, k : k + 1], scale=1.0, accum_out=total[n, u][:, k : k + 1])
 
-        def divide(n, t):
-            seen = (t + 1) * P
-            share = stat.tile([P, 1], F32, name="share")
-            nc.vector.reciprocal(share[:], total[n, t][:])
-            prob[n, t] = work.tile([P, T], BF16, name="prob")
-            nc.gpsimd.tensor_scalar(prob[n, t][:, :seen], weight[n, t][:, :seen], share[:], 1.0, MULT, MULT)
+        def divide(n, u):
+            share = stat.tile([P, len(UNITS[u])], F32, name="share")
+            nc.vector.reciprocal(share[:], total[n, u][:])
+            prob[n, u] = work.tile([P, T], BF16, name="prob")
+            for k, t in enumerate(UNITS[u]):
+                nc.gpsimd.tensor_scalar(prob[n, u][:, seen(t)], weight[n, u][:, seen(t)], share[:, k : k + 1], 1.0,
+                                        MULT, MULT)
 
-        def flip(n, t):
-            seen = (t + 1) * P
+        def flip(n, u):
             flipped = flip_pool.tile([P, T], BF16, name="flipped")
-            for i in range(t + 1):
-                nc.tensor.transpose(flipped[:, block(i)], prob[n, t][:, block(i)], ident[:])
-            prob_t[n, t] = work.tile([P, T], BF16, name="prob_t")
-            nc.vector.tensor_copy(prob_t[n, t][:, :seen], flipped[:, :seen])
+            blocks_seen = sum(t + 1 for t in UNITS[u])
+            for i in range(blocks_seen):
+                nc.tensor.transpose(flipped[:, block(i)], prob[n, u][:, block(i)], ident[:])
+            prob_t[n, u] = work.tile([P, T], BF16, name="prob_t")
+            nc.vector.tensor_copy(prob_t[n, u][:, : blocks_seen * P], flipped[:, : blocks_seen * P])
 
-        def mix(n, t):
+        def mix(n, u):
             b, h = divmod(n, H)
-            if t == TB - 1:
+            if u == 0:
                 mixed[n] = mix_pool.tile([P, T], F32, name="mixed")
-            for i in range(t + 1):
-                nc.tensor.matmul(mixed[n][:, block(t)], lhsT=val_t[b][:, i, block(h)],
-                                 rhs=prob_t[n, t][:, block(i)], start=(i == 0), stop=(i == t))
+            for t in UNITS[u]:
+                for i in range(t + 1):
+                    weights = prob_t[n, u][:, FIRST[t] + i * P : FIRST[t] + (i + 1) * P]
+                    nc.tensor.matmul(mixed[n][:, block(t)], lhsT=val_t[b][:, i, block(h)], rhs=weights,
+                                     start=(i == 0), stop=(i == t))
             if n == LAST_HEAD:
-                done = block(t)
-            elif t == 0:
+                done = tokens_of(u)
+            elif u == len(UNITS) - 1:
                 done = slice(0, T)
             else:
                 return
             nc.scalar.activation(o_bf[b][:, h, done], mixed[n][:, done], ACT.Identity,
                                  bias=bv_sb[:, h : h + 1], scale=1.0)
 
-        def ride(n, t):
+        def tokens_of(u):
+            return slice(UNITS[u][-1] * P, (UNITS[u][0] + 1) * P)
+
+        def ride(n, u):
             b, h = divmod(n, H)
-            turn = TB - 1 - t
             if b + 1 < B:
-                if turn == 0:
+                if u == 0:
                     queries(n + H)
-                if turn == 1:
+                if u == 1:
                     keys(n + H)
-                if turn == 2:
+                if u == 2:
                     values(b + 1, h)
-                if turn == 3 and b + 2 < B:
-                    look_up(b + 2, h)
-                    round_x(b + 2, h)
-            elif turn < 3:
-                earlier, a = divmod(3 * h + turn, EB)
+                    if b + 2 < B:
+                        look_up(b + 2, h)
+                        round_x(b + 2, h)
+            else:
+                earlier, a = divmod(len(UNITS) * h + u, EB)
                 finish(earlier, slice(0, T), [a])
 
         val_t[0] = sequence.tile([P, TB, E], BF16, name="val_t")
@@ -234,19 +246,18 @@ def tile_sakt_b_kernel(tc, table, pos, wq, bq, wk, wv, bv, wo, bo, offs, out):
             look_up(1, h)
             round_x(1, h)
 
-        query_blocks = [(n, t) for n in range(B * H) for t in reversed(range(TB))]
-        DIVIDE_AFTER, FLIP_AFTER, MIX_AFTER, FINISH_AFTER = 2, 4, 6, 7
-        blocks = len(query_blocks)
-        for s in range(blocks + FINISH_AFTER):
-            if s < blocks:
-                weigh(*query_blocks[s])
-            if 0 <= s - DIVIDE_AFTER < blocks:
-                divide(*query_blocks[s - DIVIDE_AFTER])
-            if 0 <= s - FLIP_AFTER < blocks:
-                flip(*query_blocks[s - FLIP_AFTER])
-            if 0 <= s - MIX_AFTER < blocks:
-                mix(*query_blocks[s - MIX_AFTER])
-            if s < blocks:
-                ride(*query_blocks[s])
-            if s - FINISH_AFTER >= blocks - TB:
-                finish(B - 1, block(query_blocks[s - FINISH_AFTER][1]), range(EB))
+        units = [(n, u) for n in range(B * H) for u in range(len(UNITS))]
+        DIVIDE_AFTER, FLIP_AFTER, MIX_AFTER, FINISH_AFTER = 1, 3, 4, 5
+        for s in range(len(units) + FINISH_AFTER):
+            if s < len(units):
+                weigh(*units[s])
+            if 0 <= s - DIVIDE_AFTER < len(units):
+                divide(*units[s - DIVIDE_AFTER])
+            if 0 <= s - FLIP_AFTER < len(units):
+                flip(*units[s - FLIP_AFTER])
+            if 0 <= s - MIX_AFTER < len(units):
+                mix(*units[s - MIX_AFTER])
+            if s < len(units):
+                ride(*units[s])
+            if s - FINISH_AFTER >= len(units) - len(UNITS):
+                finish(B - 1, tokens_of(units[s - FINISH_AFTER][1]), range(EB))

@@ -176,6 +176,7 @@ def tile_sakt_b_kernel(tc, table, pos, wq, bq, wk, wv, bv, wo, bo, offs, out):
             total[n, u] = stat.tile([P, len(UNITS[u])], F32, name="total")
             for k, t in enumerate(UNITS[u]):
                 nc.vector.reduce_max(neg_max[:, k : k + 1], score[:, seen(t)], axis=ALONG_FREE, negate=True)
+            for k, t in enumerate(UNITS[u]):
                 nc.scalar.activation(weight[n, u][:, seen(t)], score[:, seen(t)], ACT.Exp,
                                      bias=neg_max[:, k : k + 1], scale=1.0, accum_out=total[n, u][:, k : k + 1])
 
@@ -247,7 +248,7 @@ def tile_sakt_b_kernel(tc, table, pos, wq, bq, wk, wv, bv, wo, bo, offs, out):
             round_x(1, h)
 
         units = [(n, u) for n in range(B * H) for u in range(len(UNITS))]
-        DIVIDE_AFTER, FLIP_AFTER, MIX_AFTER, FINISH_AFTER = 1, 3, 4, 5
+        DIVIDE_AFTER, FLIP_AFTER, MIX_AFTER, FINISH_AFTER = 2, 3, 4, 5
         for s in range(len(units) + FINISH_AFTER):
             if s < len(units):
                 weigh(*units[s])

@@ -248,7 +248,7 @@ def tile_sakt_b_kernel(tc, table, pos, wq, bq, wk, wv, bv, wo, bo, offs, out):
             round_x(1, h)
 
         units = [(n, u) for n in range(B * H) for u in range(len(UNITS))]
-        DIVIDE_AFTER, FLIP_AFTER, MIX_AFTER, FINISH_AFTER = 2, 3, 4, 5
+        DIVIDE_AFTER, FLIP_AFTER, MIX_AFTER, FINISH_AFTER = 2, 4, 5, 6
         for s in range(len(units) + FINISH_AFTER):
             if s < len(units):
                 weigh(*units[s])

@@ -7,6 +7,7 @@ F32 = mybir.dt.float32
 BF16 = mybir.dt.bfloat16
 U16 = mybir.dt.uint16
 ADD = mybir.AluOpType.add
+MAX = mybir.AluOpType.max
 MULT = mybir.AluOpType.mult
 IS_GE = mybir.AluOpType.is_ge
 ACT = mybir.ActivationFunctionType
@@ -34,6 +35,7 @@ def tile_sakt_b_kernel(tc, table, pos, wq, bq, wk, wv, bv, wo, bo, offs, out):
         tc.tile_pool(name="sequence", bufs=3) as sequence,
         tc.tile_pool(name="work", bufs=6) as work,
         tc.tile_pool(name="stat", bufs=6) as stat,
+        tc.tile_pool(name="leaving", bufs=8) as leaving,
         tc.psum_pool(name="sum_pool", bufs=4) as sum_pool,
         tc.psum_pool(name="flip_pool", bufs=2) as flip_pool,
         tc.psum_pool(name="mix_pool", bufs=2) as mix_pool,
@@ -134,22 +136,46 @@ def tile_sakt_b_kernel(tc, table, pos, wq, bq, wk, wv, bv, wo, bo, offs, out):
                 key[b] = sequence.tile([P, H, T], BF16, name="key")
             nc.scalar.copy(key[b][:, h, :], project(wk_sb, n)[:])
 
-        def finish(b, tokens, feature_blocks):
-            width = tokens.stop - tokens.start
-            acc = {}
-            for a in feature_blocks:
-                acc[a] = sum_pool.tile([P, T], F32, name="acc", tag="sum")
-                for h in range(H - 1):
-                    nc.tensor.matmul(acc[a][:, :width], lhsT=wo_sb[:, h, block(a)], rhs=o_bf[b][:, h, tokens],
-                                     start=(h == 0), stop=False)
-            for a in feature_blocks:
-                nc.tensor.matmul(acc[a][:, :width], lhsT=wo_sb[:, H - 1, block(a)], rhs=o_bf[b][:, H - 1, tokens],
-                                 start=False, stop=True)
-                gain = work.tile([P, T], F32, name="gain")
-                nc.scalar.activation(gain[:, :width], acc[a][:, :width], ACT.Relu, bias=bo_sb[:, a : a + 1], scale=1.0)
-                y = work.tile([P, T], F32, name="y")
-                nc.vector.tensor_tensor(y[:, :width], gain[:, :width], x[b][a][:, tokens], ADD)
-                nc.sync.dma_start(out[block(a), b * T + tokens.start : b * T + tokens.stop], y[:, :width])
+        def finish(b, a):
+            acc = sum_pool.tile([P, T], F32, name="acc", tag="sum")
+            for h in range(H):
+                nc.tensor.matmul(acc[:], lhsT=wo_sb[:, h, block(a)], rhs=o_bf[b][:, h, :],
+                                 start=(h == 0), stop=(h == H - 1))
+            gain = work.tile([P, T], F32, name="gain")
+            nc.scalar.activation(gain[:], acc[:], ACT.Relu, bias=bo_sb[:, a : a + 1], scale=1.0)
+            y = leaving.tile([P, T], F32, name="y")
+            nc.vector.tensor_tensor(y[:], gain[:], x[b][a][:], ADD)
+            nc.sync.dma_start(out[block(a), b * T : (b + 1) * T], y[:])
+
+        HALF = T // 2
+        last_sum = {}
+
+        def add_share(h, half, tokens, closes=False):
+            o_head = o_bf[B - 1][:, h, half * HALF + tokens.start : half * HALF + tokens.stop]
+            for a in range(EB):
+                pair, place = divmod(a, 2)
+                if h == 0 and place == 0:
+                    last_sum[half, pair] = sum_pool.tile([P, 2, HALF], F32, name="acc", tag="sum")
+                nc.tensor.matmul(last_sum[half, pair][:, place, tokens], lhsT=wo_sb[:, h, block(a)], rhs=o_head,
+                                 start=(h == 0 and place == 0), stop=(closes and place == 1))
+
+        def add_head(h):
+            for half in (1, 0):
+                add_share(h, half, slice(0, HALF))
+
+        def add_last_head(u):
+            half = 1 if u < 2 else 0
+            tokens = slice(tokens_of(u).start - half * HALF, tokens_of(u).stop - half * HALF)
+            add_share(H - 1, half, tokens, closes=(u > 0))
+            if u == 0:
+                return
+            for a in range(EB):
+                pair, place = divmod(a, 2)
+                y = leaving.tile([P, T], F32, name="y")
+                nc.vector.scalar_tensor_tensor(y[:, :HALF], last_sum[half, pair][:, place, :], neg_bo[:, a : a + 1],
+                                               x[B - 1][a][:, half * HALF : (half + 1) * HALF], MAX, ADD)
+                first = (B - 1) * T + half * HALF
+                nc.sync.dma_start(out[block(a), first : first + HALF], y[:, :HALF])
 
         UNITS = [[3], [2], [1, 0]]
         FIRST = {3: 0, 2: 0, 1: 0, 0: 2 * P}
@@ -229,9 +255,12 @@ def tile_sakt_b_kernel(tc, table, pos, wq, bq, wk, wv, bv, wo, bo, offs, out):
                     if b + 2 < B:
                         look_up(b + 2, h)
                         round_x(b + 2, h)
+                if (b + 2, u) == (B, 2):
+                    if h == 0:
+                        nc.vector.tensor_scalar(neg_bo[:], bo_sb[:], -1.0, None, MULT)
+                    nc.vector.tensor_scalar(x[B - 1][h][:], x[B - 1][h][:], bo_sb[:, h : h + 1], None, ADD)
             else:
-                earlier, a = divmod(len(UNITS) * h + u, EB)
-                finish(earlier, slice(0, T), [a])
+                finish(*divmod(len(UNITS) * h + u, EB))
 
         val_t[0] = sequence.tile([P, TB, E], BF16, name="val_t")
         for c in range(EB):
@@ -241,6 +270,7 @@ def tile_sakt_b_kernel(tc, table, pos, wq, bq, wk, wv, bv, wo, bo, offs, out):
                 values_part(0, i, c)
         bq_scaled = held.tile([P, H], F32, name="bq_scaled")
         nc.vector.tensor_scalar(bq_scaled[:], bq_sb[:], SCALE, None, MULT)
+        neg_bo = held.tile([P, EB], F32, name="neg_bo")
         for h in range(H):
             queries(h)
             keys(h)
@@ -248,17 +278,19 @@ def tile_sakt_b_kernel(tc, table, pos, wq, bq, wk, wv, bv, wo, bo, offs, out):
             round_x(1, h)
 
         units = [(n, u) for n in range(B * H) for u in range(len(UNITS))]
-        DIVIDE_AFTER, FLIP_AFTER, MIX_AFTER, FINISH_AFTER = 2, 4, 5, 6
+        STAGES = [divide, flip, mix]
+        AFTER, LAST_AFTER = [2, 4, 5], [2, 3, 4]
+        FINISH_AFTER = LAST_AFTER[-1] + 1
         for s in range(len(units) + FINISH_AFTER):
             if s < len(units):
                 weigh(*units[s])
-            if 0 <= s - DIVIDE_AFTER < len(units):
-                divide(*units[s - DIVIDE_AFTER])
-            if 0 <= s - FLIP_AFTER < len(units):
-                flip(*units[s - FLIP_AFTER])
-            if 0 <= s - MIX_AFTER < len(units):
-                mix(*units[s - MIX_AFTER])
+            for k, stage in enumerate(STAGES):
+                for i, (n, u) in enumerate(units):
+                    if s - i == (LAST_AFTER if n == LAST_HEAD else AFTER)[k]:
+                        stage(n, u)
             if s < len(units):
                 ride(*units[s])
+            elif s - len(units) < H - 1:
+                add_head(s - len(units))
             if s - FINISH_AFTER >= len(units) - len(UNITS):
-                finish(B - 1, tokens_of(units[s - FINISH_AFTER][1]), range(EB))
+                add_last_head(units[s - FINISH_AFTER][1])

@@ -211,8 +211,12 @@ def tile_sakt_b_kernel(tc, table, pos, wq, bq, wk, wv, bv, wo, bo, offs, out):
             nc.vector.reciprocal(share[:], total[n, u][:])
             prob[n, u] = work.tile([P, T], BF16, name="prob")
             for k, t in enumerate(UNITS[u]):
-                nc.gpsimd.tensor_scalar(prob[n, u][:, seen(t)], weight[n, u][:, seen(t)], share[:, k : k + 1], 1.0,
-                                        MULT, MULT)
+                if len(UNITS[u]) == 1:
+                    nc.gpsimd.tensor_scalar(prob[n, u][:, seen(t)], weight[n, u][:, seen(t)], share[:, k : k + 1],
+                                            1.0, MULT, MULT)
+                else:
+                    nc.scalar.activation(prob[n, u][:, seen(t)], weight[n, u][:, seen(t)], ACT.Identity,
+                                         bias=0.0, scale=share[:, k : k + 1])
 
         def flip(n, u):
             flipped = flip_pool.tile([P, T], BF16, name="flipped")

import math

import concourse.mybir as mybir
from concourse.masks import make_identity

F32 = mybir.dt.float32
BF16 = mybir.dt.bfloat16
U16 = mybir.dt.uint16
ADD = mybir.AluOpType.add
MAX = mybir.AluOpType.max
MULT = mybir.AluOpType.mult
IS_GE = mybir.AluOpType.is_ge
ACT = mybir.ActivationFunctionType
ALONG_FREE = mybir.AxisListType.X

P = 128
E, V, B, T, H, D = 512, 512, 4, 512, 4, 128
N = B * T
EB = E // P
TB = T // P
SCALE = 1.0 / math.sqrt(D)
MASKED = -1.0e9

FLOPS = 8 * E * E * N + 2 * B * H * D * T * (T + 1)


def block(i):
    return slice(i * P, (i + 1) * P)


def tile_sakt_b_kernel(tc, table, pos, wq, bq, wk, wv, bv, wo, bo, offs, out):
    nc = tc.nc
    with (
        tc.tile_pool(name="held", bufs=1) as held,
        tc.tile_pool(name="sequence", bufs=3) as sequence,
        tc.tile_pool(name="work", bufs=6) as work,
        tc.tile_pool(name="stat", bufs=6) as stat,
        tc.tile_pool(name="leaving", bufs=8) as leaving,
        tc.psum_pool(name="sum_pool", bufs=4) as sum_pool,
        tc.psum_pool(name="flip_pool", bufs=2) as flip_pool,
        tc.psum_pool(name="mix_pool", bufs=2) as mix_pool,
    ):
        offsets = held.tile([P, N // 16], U16, name="offsets")
        nc.sync.dma_start(offsets[:], offs)

        def load_weight(w, name):
            w_sb = held.tile([P, EB, E], BF16, name=name)
            nc.sync.dma_start(w_sb[:], w.rearrange("(a p) m -> p a m", p=P))
            return w_sb

        def load_bias(bias, name):
            bias_sb = held.tile([P, EB], F32, name=name)
            with nc.allow_non_contiguous_dma(reason="512 single values, once"):
                nc.sync.dma_start(bias_sb[:], bias.rearrange("(a p) o -> p (a o)", p=P))
            return bias_sb

        table_sb = [held.tile([P, V], F32, name=f"table{c}") for c in range(EB)]
        pos_sb = [[held.tile([P, T], F32, name=f"pos{b}_{c}") for c in range(EB)] for b in range(B)]

        def load_pos(b, c):
            nc.sync.dma_start(pos_sb[b][c][:], pos[block(c), b * T : (b + 1) * T])

        for c in range(EB):
            nc.sync.dma_start(table_sb[c][:], table[block(c), :])
            load_pos(0, c)
            if c == 1:
                wv_sb = load_weight(wv, "wv_sb")
        bq_sb = load_bias(bq, "bq_sb")
        wq_sb = load_weight(wq, "wq_sb")
        wk_sb = load_weight(wk, "wk_sb")
        for c in range(EB):
            load_pos(1, c)
        bv_sb = load_bias(bv, "bv_sb")
        wo_sb = load_weight(wo, "wo_sb")
        bo_sb = load_bias(bo, "bo_sb")
        for b in range(2, B):
            for c in range(EB):
                load_pos(b, c)

        ident = held.tile([P, P], BF16, name="ident")
        make_identity(nc, ident[:])
        future = held.tile([P, P], BF16, name="future")
        nc.gpsimd.memset(future[:], 0.0)
        nc.gpsimd.affine_select(
            out=future[:], in_=future[:], pattern=[[-1, P]], compare_op=IS_GE,
            fill=MASKED, base=0, channel_multiplier=1,
        )

        x = [[held.tile([P, T], F32, name=f"x{b}_{c}") for c in range(EB)] for b in range(B)]
        x_bf = [held.tile([P, EB, T], BF16, name=f"x_bf{b}") for b in range(B)]
        o_bf = [held.tile([P, H, T], BF16, name=f"o_bf{b}") for b in range(B)]
        val_t = {}
        qry = {}
        key = {}
        val_sum = {}

        def look_up(b, c):
            picked = table_sb[c][:].indirect(offsets[:, b * (T // 16) : (b + 1) * (T // 16)])
            nc.vector.tensor_tensor(x[b][c][:], picked, pos_sb[b][c][:], ADD)

        def round_x(b, c):
            nc.scalar.copy(x_bf[b][:, c, :], x[b][c][:])

        def values_part(b, i, c):
            if c == 0:
                val_sum[b, i] = sum_pool.tile([P, E], F32, name="acc", tag="sum")
            nc.tensor.matmul(val_sum[b, i][:], lhsT=x_bf[b][:, c, block(i)], rhs=wv_sb[:, c, :],
                             start=(c == 0), stop=(c == EB - 1))
            if c == EB - 1:
                nc.scalar.copy(val_t[b][:, i, :], val_sum[b, i][:])

        def values(b, i):
            if i == 0:
                val_t[b] = sequence.tile([P, TB, E], BF16, name="val_t")
            for c in range(EB):
                values_part(b, i, c)

        def project(w_sb, n):
            b, h = divmod(n, H)
            acc = sum_pool.tile([P, T], F32, name="acc", tag="sum")
            for c in range(EB):
                nc.tensor.matmul(acc[:], lhsT=w_sb[:, c, block(h)], rhs=x_bf[b][:, c, :],
                                 start=(c == 0), stop=(c == EB - 1))
            return acc

        def queries(n):
            b, h = divmod(n, H)
            if h == 0:
                qry[b] = sequence.tile([P, H, T], BF16, name="qry")
            nc.scalar.activation(qry[b][:, h, :], project(wq_sb, n)[:], ACT.Identity,
                                 bias=bq_scaled[:, h : h + 1], scale=SCALE)

        def keys(n):
            b, h = divmod(n, H)
            if h == 0:
                key[b] = sequence.tile([P, H, T], BF16, name="key")
            nc.scalar.copy(key[b][:, h, :], project(wk_sb, n)[:])

        def finish(b, a):
            acc = sum_pool.tile([P, T], F32, name="acc", tag="sum")
            for h in range(H):
                nc.tensor.matmul(acc[:], lhsT=wo_sb[:, h, block(a)], rhs=o_bf[b][:, h, :],
                                 start=(h == 0), stop=(h == H - 1))
            gain = work.tile([P, T], F32, name="gain")
            nc.scalar.activation(gain[:], acc[:], ACT.Relu, bias=bo_sb[:, a : a + 1], scale=1.0)
            y = leaving.tile([P, T], F32, name="y")
            nc.vector.tensor_tensor(y[:], gain[:], x[b][a][:], ADD)
            nc.sync.dma_start(out[block(a), b * T : (b + 1) * T], y[:])

        HALF = T // 2
        last_sum = {}

        def add_share(h, half, tokens, closes=False):
            o_head = o_bf[B - 1][:, h, half * HALF + tokens.start : half * HALF + tokens.stop]
            for a in range(EB):
                pair, place = divmod(a, 2)
                if h == 0 and place == 0:
                    last_sum[half, pair] = sum_pool.tile([P, 2, HALF], F32, name="acc", tag="sum")
                nc.tensor.matmul(last_sum[half, pair][:, place, tokens], lhsT=wo_sb[:, h, block(a)], rhs=o_head,
                                 start=(h == 0 and place == 0), stop=(closes and place == 1))

        def add_head(h):
            for half in (1, 0):
                add_share(h, half, slice(0, HALF))

        def add_last_head(u):
            half = 1 if u < 2 else 0
            tokens = slice(tokens_of(u).start - half * HALF, tokens_of(u).stop - half * HALF)
            add_share(H - 1, half, tokens, closes=(u > 0))
            if u == 0:
                return
            for a in range(EB):
                pair, place = divmod(a, 2)
                y = leaving.tile([P, T], F32, name="y")
                nc.vector.scalar_tensor_tensor(y[:, :HALF], last_sum[half, pair][:, place, :], neg_bo[:, a : a + 1],
                                               x[B - 1][a][:, half * HALF : (half + 1) * HALF], MAX, ADD)
                first = (B - 1) * T + half * HALF
                nc.sync.dma_start(out[block(a), first : first + HALF], y[:, :HALF])

        UNITS = [[3], [2], [1, 0]]
        FIRST = {3: 0, 2: 0, 1: 0, 0: 2 * P}
        weight = {}
        total = {}
        prob = {}
        prob_t = {}
        mixed = {}
        LAST_HEAD = B * H - 1

        def seen(t):
            return slice(FIRST[t], FIRST[t] + (t + 1) * P)

        def weigh(n, u):
            b, h = divmod(n, H)
            score = sum_pool.tile([P, T], F32, name="score", tag="sum")
            for t in UNITS[u]:
                nc.tensor.matmul(score[:, seen(t)], lhsT=qry[b][:, h, block(t)], rhs=key[b][:, h, : (t + 1) * P],
                                 start=True, stop=False)
                own = slice(seen(t).stop - P, seen(t).stop)
                nc.tensor.matmul(score[:, own], lhsT=ident[:], rhs=future[:], start=False, stop=True)
            neg_max = stat.tile([P, len(UNITS[u])], F32, name="neg_max")
            weight[n, u] = work.tile([P, T], BF16, name="weight")
            total[n, u] = stat.tile([P, len(UNITS[u])], F32, name="total")
            for k, t in enumerate(UNITS[u]):
                nc.vector.reduce_max(neg_max[:, k : k + 1], score[:, seen(t)], axis=ALONG_FREE, negate=True)
            for k, t in enumerate(UNITS[u]):
                nc.scalar.activation(weight[n, u][:, seen(t)], score[:, seen(t)], ACT.Exp,
                                     bias=neg_max[:, k : k + 1], scale=1.0, accum_out=total[n, u][:, k : k + 1])

        def divide(n, u):
            share = stat.tile([P, len(UNITS[u])], F32, name="share")
            nc.vector.reciprocal(share[:], total[n, u][:])
            prob[n, u] = work.tile([P, T], BF16, name="prob")
            for k, t in enumerate(UNITS[u]):
                if len(UNITS[u]) == 1:
                    nc.gpsimd.tensor_scalar(prob[n, u][:, seen(t)], weight[n, u][:, seen(t)], share[:, k : k + 1],
                                            1.0, MULT, MULT)
                else:
                    nc.scalar.activation(prob[n, u][:, seen(t)], weight[n, u][:, seen(t)], ACT.Identity,
                                         bias=0.0, scale=share[:, k : k + 1])

        def flip(n, u):
            flipped = flip_pool.tile([P, T], BF16, name="flipped")
            blocks_seen = sum(t + 1 for t in UNITS[u])
            for i in range(blocks_seen):
                nc.tensor.transpose(flipped[:, block(i)], prob[n, u][:, block(i)], ident[:])
            prob_t[n, u] = work.tile([P, T], BF16, name="prob_t")
            nc.vector.tensor_copy(prob_t[n, u][:, : blocks_seen * P], flipped[:, : blocks_seen * P])

        def mix(n, u):
            b, h = divmod(n, H)
            if u == 0:
                mixed[n] = mix_pool.tile([P, T], F32, name="mixed")
            for t in UNITS[u]:
                for i in range(t + 1):
                    weights = prob_t[n, u][:, FIRST[t] + i * P : FIRST[t] + (i + 1) * P]
                    nc.tensor.matmul(mixed[n][:, block(t)], lhsT=val_t[b][:, i, block(h)], rhs=weights,
                                     start=(i == 0), stop=(i == t))
            if n == LAST_HEAD:
                done = tokens_of(u)
            elif u == len(UNITS) - 1:
                done = slice(0, T)
            else:
                return
            nc.scalar.activation(o_bf[b][:, h, done], mixed[n][:, done], ACT.Identity,
                                 bias=bv_sb[:, h : h + 1], scale=1.0)

        def tokens_of(u):
            return slice(UNITS[u][-1] * P, (UNITS[u][0] + 1) * P)

        def ride(n, u):
            b, h = divmod(n, H)
            if b + 1 < B:
                if u == 0:
                    queries(n + H)
                if u == 1:
                    keys(n + H)
                if u == 2:
                    values(b + 1, h)
                    if b + 2 < B:
                        look_up(b + 2, h)
                        round_x(b + 2, h)
                if (b + 2, u) == (B, 2):
                    if h == 0:
                        nc.vector.tensor_scalar(neg_bo[:], bo_sb[:], -1.0, None, MULT)
                    nc.vector.tensor_scalar(x[B - 1][h][:], x[B - 1][h][:], bo_sb[:, h : h + 1], None, ADD)
            else:
                finish(*divmod(len(UNITS) * h + u, EB))

        val_t[0] = sequence.tile([P, TB, E], BF16, name="val_t")
        for c in range(EB):
            look_up(0, c)
            round_x(0, c)
            for i in range(TB):
                values_part(0, i, c)
        bq_scaled = held.tile([P, H], F32, name="bq_scaled")
        nc.vector.tensor_scalar(bq_scaled[:], bq_sb[:], SCALE, None, MULT)
        neg_bo = held.tile([P, EB], F32, name="neg_bo")
        for h in range(H):
            queries(h)
            keys(h)
            look_up(1, h)
            round_x(1, h)

        units = [(n, u) for n in range(B * H) for u in range(len(UNITS))]
        STAGES = [divide, flip, mix]
        AFTER, LAST_AFTER = [2, 4, 5], [2, 3, 4]
        FINISH_AFTER = LAST_AFTER[-1] + 1
        for s in range(len(units) + FINISH_AFTER):
            if s < len(units):
                weigh(*units[s])
            for k, stage in enumerate(STAGES):
                for i, (n, u) in enumerate(units):
                    if s - i == (LAST_AFTER if n == LAST_HEAD else AFTER)[k]:
                        stage(n, u)
            if s < len(units):
                ride(*units[s])
            elif s - len(units) < H - 1:
                add_head(s - len(units))
            if s - FINISH_AFTER >= len(units) - len(UNITS):
                add_last_head(units[s - FINISH_AFTER][1])
